import numpy as np
import ml_dtypes

BF16 = ml_dtypes.bfloat16


def bf(x):
    return np.asarray(x, np.float32).astype(BF16)


def f32(x):
    return np.asarray(x, np.float32)


def f64(x):
    return np.asarray(x).astype(np.float64)


def striped(idx):
    return np.tile(idx.reshape(-1, 16).T, (8, 1))


C, S, N = 128, 256, 64


def setup_inputs():
    return {"base": f32(np.random.standard_normal((C, S))), "e_par": f32(np.random.standard_normal((C, N))), "left": f32(np.random.standard_normal((C, N))), "right": f32(np.random.standard_normal((C, N))), "offs": striped(np.random.permutation(S)[:N])}


def reference(base, e_par, left, right, offs):
    idx = offs[:16].T.reshape(-1)
    res = f64(base).copy()
    res[:, idx] = f64(e_par) + (f64(left) + f64(right))
    return res

@@ -1,0 +1,32 @@
+import concourse.mybir as mybir
+
+F32 = mybir.dt.float32
+U16 = mybir.dt.uint16
+ADD = mybir.AluOpType.add
+
+FEATURES = 128
+SLOTS = 256
+LISTED = 64
+OFFSETS_PER_COLUMN = 16
+
+
+def tile_batchprogramclassifier_s_kernel(tc, base, e_par, left, right, offs, out):
+    nc = tc.nc
+    with tc.tile_pool(name="held", bufs=1) as held:
+        offsets = held.tile([FEATURES, LISTED // OFFSETS_PER_COLUMN], U16, name="offsets")
+        window = held.tile([FEATURES, SLOTS], F32, name="window")
+        parents = held.tile([FEATURES, LISTED], F32, name="parents")
+        left_kids = held.tile([FEATURES, LISTED], F32, name="left_kids")
+        right_kids = held.tile([FEATURES, LISTED], F32, name="right_kids")
+        kids_sum = held.tile([FEATURES, LISTED], F32, name="kids_sum")
+
+        nc.sync.dma_start(offsets[:], offs)
+        nc.sync.dma_start(left_kids[:], left)
+        nc.sync.dma_start(right_kids[:], right)
+        nc.sync.dma_start(parents[:], e_par)
+        nc.sync.dma_start(window[:], base)
+
+        nc.vector.tensor_tensor(kids_sum[:], left_kids[:], right_kids[:], ADD)
+        nc.vector.tensor_tensor(window[:].indirect(offsets[:]), parents[:], kids_sum[:], ADD)
+
+        nc.sync.dma_start(out, window[:])

@@ -8,17 +8,18 @@ FEATURES = 128
 SLOTS = 256
 LISTED = 64
 OFFSETS_PER_COLUMN = 16
+BURST = 256
 
 
 def tile_batchprogramclassifier_s_kernel(tc, base, e_par, left, right, offs, out):
     nc = tc.nc
     with tc.tile_pool(name="held", bufs=1) as held:
-        offsets = held.tile([FEATURES, LISTED // OFFSETS_PER_COLUMN], U16, name="offsets")
-        window = held.tile([FEATURES, SLOTS], F32, name="window")
-        parents = held.tile([FEATURES, LISTED], F32, name="parents")
-        left_kids = held.tile([FEATURES, LISTED], F32, name="left_kids")
-        right_kids = held.tile([FEATURES, LISTED], F32, name="right_kids")
+        window = held.tile([FEATURES, SLOTS], F32, name="window", align_bytes=BURST)
+        parents = held.tile([FEATURES, LISTED], F32, name="parents", align_bytes=BURST)
+        left_kids = held.tile([FEATURES, LISTED], F32, name="left_kids", align_bytes=BURST)
+        right_kids = held.tile([FEATURES, LISTED], F32, name="right_kids", align_bytes=BURST)
         kids_sum = held.tile([FEATURES, LISTED], F32, name="kids_sum")
+        offsets = held.tile([FEATURES, LISTED // OFFSETS_PER_COLUMN], U16, name="offsets")
 
         nc.sync.dma_start(offsets[:], offs)
         nc.sync.dma_start(left_kids[:], left)

@@ -21,11 +21,11 @@ def tile_batchprogramclassifier_s_kernel(tc, base, e_par, left, right, offs, out
         kids_sum = held.tile([FEATURES, LISTED], F32, name="kids_sum")
         offsets = held.tile([FEATURES, LISTED // OFFSETS_PER_COLUMN], U16, name="offsets")
 
-        nc.sync.dma_start(offsets[:], offs)
         nc.sync.dma_start(left_kids[:], left)
         nc.sync.dma_start(right_kids[:], right)
-        nc.sync.dma_start(parents[:], e_par)
         nc.sync.dma_start(window[:], base)
+        nc.sync.dma_start(offsets[:], offs)
+        nc.sync.dma_start(parents[:], e_par)
 
         nc.vector.tensor_tensor(kids_sum[:], left_kids[:], right_kids[:], ADD)
         nc.vector.tensor_tensor(window[:].indirect(offsets[:]), parents[:], kids_sum[:], ADD)

@@ -24,8 +24,8 @@ def tile_batchprogramclassifier_s_kernel(tc, base, e_par, left, right, offs, out
         nc.sync.dma_start(left_kids[:], left)
         nc.sync.dma_start(right_kids[:], right)
         nc.sync.dma_start(window[:], base)
-        nc.sync.dma_start(offsets[:], offs)
         nc.sync.dma_start(parents[:], e_par)
+        nc.sync.dma_start(offsets[:], offs)
 
         nc.vector.tensor_tensor(kids_sum[:], left_kids[:], right_kids[:], ADD)
         nc.vector.tensor_tensor(window[:].indirect(offsets[:]), parents[:], kids_sum[:], ADD)

@@ -23,8 +23,8 @@ def tile_batchprogramclassifier_s_kernel(tc, base, e_par, left, right, offs, out
 
         nc.sync.dma_start(left_kids[:], left)
         nc.sync.dma_start(right_kids[:], right)
+        nc.scalar.dma_start(parents[:], e_par)
         nc.sync.dma_start(window[:], base)
-        nc.sync.dma_start(parents[:], e_par)
         nc.sync.dma_start(offsets[:], offs)
 
         nc.vector.tensor_tensor(kids_sum[:], left_kids[:], right_kids[:], ADD)

@@ -23,8 +23,8 @@ def tile_batchprogramclassifier_s_kernel(tc, base, e_par, left, right, offs, out
 
         nc.sync.dma_start(left_kids[:], left)
         nc.sync.dma_start(right_kids[:], right)
+        nc.scalar.dma_start(window[:], base)
         nc.scalar.dma_start(parents[:], e_par)
-        nc.sync.dma_start(window[:], base)
         nc.sync.dma_start(offsets[:], offs)
 
         nc.vector.tensor_tensor(kids_sum[:], left_kids[:], right_kids[:], ADD)

@@ -22,8 +22,8 @@ def tile_batchprogramclassifier_s_kernel(tc, base, e_par, left, right, offs, out
         offsets = held.tile([FEATURES, LISTED // OFFSETS_PER_COLUMN], U16, name="offsets")
 
         nc.sync.dma_start(left_kids[:], left)
-        nc.sync.dma_start(right_kids[:], right)
-        nc.scalar.dma_start(window[:], base)
+        nc.scalar.dma_start(right_kids[:], right)
+        nc.sync.dma_start(window[:], base)
         nc.scalar.dma_start(parents[:], e_par)
         nc.sync.dma_start(offsets[:], offs)
 

@@ -23,9 +23,9 @@ def tile_batchprogramclassifier_s_kernel(tc, base, e_par, left, right, offs, out
 
         nc.sync.dma_start(left_kids[:], left)
         nc.scalar.dma_start(right_kids[:], right)
-        nc.sync.dma_start(window[:], base)
-        nc.scalar.dma_start(parents[:], e_par)
         nc.sync.dma_start(offsets[:], offs)
+        nc.scalar.dma_start(parents[:], e_par)
+        nc.sync.dma_start(window[:], base)
 
         nc.vector.tensor_tensor(kids_sum[:], left_kids[:], right_kids[:], ADD)
         nc.vector.tensor_tensor(window[:].indirect(offsets[:]), parents[:], kids_sum[:], ADD)

import concourse.mybir as mybir

F32 = mybir.dt.float32
U16 = mybir.dt.uint16
ADD = mybir.AluOpType.add

FEATURES = 128
SLOTS = 256
LISTED = 64
OFFSETS_PER_COLUMN = 16
BURST = 256


def tile_batchprogramclassifier_s_kernel(tc, base, e_par, left, right, offs, out):
    nc = tc.nc
    with tc.tile_pool(name="held", bufs=1) as held:
        window = held.tile([FEATURES, SLOTS], F32, name="window", align_bytes=BURST)
        parents = held.tile([FEATURES, LISTED], F32, name="parents", align_bytes=BURST)
        left_kids = held.tile([FEATURES, LISTED], F32, name="left_kids", align_bytes=BURST)
        right_kids = held.tile([FEATURES, LISTED], F32, name="right_kids", align_bytes=BURST)
        kids_sum = held.tile([FEATURES, LISTED], F32, name="kids_sum")
        offsets = held.tile([FEATURES, LISTED // OFFSETS_PER_COLUMN], U16, name="offsets")

        nc.sync.dma_start(left_kids[:], left)
        nc.scalar.dma_start(right_kids[:], right)
        nc.sync.dma_start(offsets[:], offs)
        nc.scalar.dma_start(parents[:], e_par)
        nc.sync.dma_start(window[:], base)

        nc.vector.tensor_tensor(kids_sum[:], left_kids[:], right_kids[:], ADD)
        nc.vector.tensor_tensor(window[:].indirect(offsets[:]), parents[:], kids_sum[:], ADD)

        nc.sync.dma_start(out, window[:])
